import numpy as np
import ml_dtypes


def mxq(x, axis, fmt="e4m3"):
    dtype, down = {"e4m3": (ml_dtypes.float8_e4m3fn, 7), "e5m2": (ml_dtypes.float8_e5m2, 14)}[fmt]
    v = np.moveaxis(np.asarray(x, np.float32).astype(ml_dtypes.bfloat16).astype(np.float64), axis, -1)
    blocks = v.reshape(v.shape[:-1] + (-1, 32))
    amax = np.abs(blocks).max(-1, keepdims=True)
    byte = np.maximum(np.where(amax > 0, np.frexp(amax)[1] - 1 + 127, 0) - down, 1)
    scale = np.exp2(byte - 127.0)
    codes = (blocks / scale).astype(np.float32).astype(dtype).astype(np.float64)
    return np.moveaxis((codes * scale).reshape(v.shape), -1, axis)


WIDE = False


def mx_kscale(k):
    if not WIDE:
        return np.ones(k)
    levels = np.array([10, -10, 5, -5, 0])
    a = np.random.permutation(np.resize(levels, k // 512 * 4)).reshape(k // 512, 4)
    idx = np.arange(k)
    return np.exp2(a[idx // 512, idx % 128 // 32])


BF16 = ml_dtypes.bfloat16


def bf(x):
    return np.asarray(x, np.float32).astype(BF16)


def f64(x):
    return np.asarray(x).astype(np.float64)


E2M1 = np.array([0.0, 0.5, 1.0, 1.5, 2.0, 3.0, 4.0, 6.0, -0.0, -0.5, -1.0, -1.5, -2.0, -3.0, -4.0, -6.0])


def pack_weight(w, fmt):
    k, n = w.shape
    w = f64(bf(w)).reshape(k // 32, 32, n)
    amax = np.abs(w).max(1)
    if fmt == "e4m3":
        byte = np.frexp(amax)[1] - 1 + 127 - 7
    else:
        mant, ex = np.frexp(amax / 6.0)
        byte = np.where(mant > 0.5, ex, ex - 1) + 127
    byte = np.clip(np.where(amax > 0, byte, 1), 1, 254)
    scaled = (w * np.exp2(127.0 - byte)[:, None, :]).reshape(k, n).astype(np.float32)
    by_word = np.ascontiguousarray(scaled.reshape(k // 512, 128, 4, n).transpose(0, 1, 3, 2))
    if fmt == "e4m3":
        words = by_word.astype(ml_dtypes.float8_e4m3fn).view(np.uint8)
    else:
        c = by_word.astype(ml_dtypes.float4_e2m1fn).view(np.uint8) & 0xF
        words = c[..., 0::2] | (c[..., 1::2] << 4)
    return np.ascontiguousarray(words), np.ascontiguousarray(byte.astype(np.uint8).reshape(k // 512, 16, n))


def unpack_weight(words, scales, fmt):
    g, p, n, _ = words.shape
    if fmt == "e4m3":
        vals = np.ascontiguousarray(words).view(ml_dtypes.float8_e4m3fn).astype(np.float64)
    else:
        nib = np.empty((g, p, n, 4), np.uint8)
        nib[..., 0::2] = words & 0xF
        nib[..., 1::2] = words >> 4
        vals = E2M1[nib]
    vals = vals * np.repeat(np.exp2(scales.astype(np.float64) - 127.0), 8, axis=1)[..., None]
    return vals.transpose(0, 1, 3, 2).reshape(g * 512, n)


B, DIM, HID, H, SEQ, DOUT = 128, 4096, 2048, 2, 2048, 2048
DECAY_CONSTANT = SEQ // 512
H2 = H // 2
F = H * HID


def setup_inputs():
    s = mx_kscale(DIM)
    x = bf(np.random.standard_normal((B, DIM)) * s)
    W_proj = bf(np.random.standard_normal((H, DIM, HID)) / np.sqrt(DIM) / s[:, None])
    b_proj = bf(np.random.standard_normal((H, HID)) * 0.1)
    W_out_words, W_out_scales = pack_weight(np.random.standard_normal((F, DOUT)) / np.sqrt(F), "e4m3")
    b_out = bf(np.random.standard_normal(DOUT) * 0.1)
    w_mix = bf(np.concatenate([0.4 + 0.05 * np.random.standard_normal((H2, SEQ)), -0.3 + 0.05 * np.random.standard_normal((H - H2, SEQ))], axis=0))
    b_mix = bf(np.concatenate([3.0 + 0.1 * np.random.standard_normal((H2, SEQ)), 0.2 + 0.1 * np.random.standard_normal((H - H2, SEQ))], axis=0))
    decay_values = bf(0.95 + 0.05 * np.random.standard_normal(H))
    caches = bf(np.random.standard_normal((H, B, HID)))
    return {"x": x, "index": 7, "W_proj": W_proj, "b_proj": b_proj, "W_out_words": W_out_words, "W_out_scales": W_out_scales, "b_out": b_out,
            "w_mix": w_mix, "b_mix": b_mix, "decay_values": decay_values, "caches": caches}


def reference(x, index, W_proj, b_proj, W_out_words, W_out_scales, b_out, w_mix, b_mix, decay_values, caches):
    proj = (mxq(f64(x), 1, "e4m3") @ mxq(f64(W_proj), 1, "e4m3")) + f64(b_proj)[:, None, :]
    decay = np.clip(f64(decay_values), 0.9, 1.0) ** (1.0 / DECAY_CONSTANT)
    w = f64(w_mix)[:, index]
    b = f64(b_mix)[:, index]
    cache_coef = np.concatenate([w[:H2] * decay[:H2], decay[H2:]], axis=0)
    out = (w[:, None, None] * proj
           + cache_coef[:, None, None] * f64(caches)
           + b[:, None, None])
    hidden = np.transpose(out, (1, 0, 2)).reshape(B, H * HID)
    return (mxq(hidden, 1, "e4m3") @ unpack_weight(W_out_words, W_out_scales, "e4m3")) + f64(b_out)

@@ -1,0 +1,385 @@
+from contextlib import ExitStack
+
+import concourse.mybir as mybir
+from concourse.masks import make_identity
+
+FP8X4 = mybir.dt.float8_e4m3fn_x4
+BF16 = mybir.dt.bfloat16
+F32 = mybir.dt.float32
+I32 = mybir.dt.int32
+U32 = mybir.dt.uint32
+U8 = mybir.dt.uint8
+ALU = mybir.AluOpType
+ACT = mybir.ActivationFunctionType
+
+P = 128
+PACK = 4
+KP = P * PACK
+B, DIM, HID, H, DOUT = 128, 4096, 2048, 2, 2048
+NB = 512
+PASSES = DIM // KP
+NCH = H * PASSES
+HALF = HID // 2
+RING = 7
+NPAIR = 4
+V_LIGHT = (5, 8, 12)
+ONES_ROW = 32
+
+FLOPS = 2 * B * DIM * H * HID + 2 * B * H * HID * DOUT
+
+
+def tile_mixedrepeatheads_w_kernel(
+    tc, x, index, W_proj, b_proj, W_out_words, W_out_scales, b_out, w_mix, b_mix, decay_values, caches, out
+):
+    nc = tc.nc
+    with ExitStack() as ctx:
+        const = ctx.enter_context(tc.tile_pool(name="const", bufs=1))
+        ring = ctx.enter_context(tc.tile_pool(name="ring", bufs=RING))
+        grp = ctx.enter_context(tc.tile_pool(name="grp", bufs=8))
+        cod = ctx.enter_context(tc.tile_pool(name="cod", bufs=6))
+        act = ctx.enter_context(tc.tile_pool(name="act", bufs=1))
+        tpool = ctx.enter_context(tc.tile_pool(name="tpool", bufs=2))
+        psum = ctx.enter_context(tc.psum_pool(name="psum", bufs=1))
+        ctx.enter_context(tc.manual_schedule())
+
+        warm = const.tile([P, 1], F32, name="warm")
+        warm2 = const.tile([P, 1], F32, name="warm2")
+        nc.vector.memset(warm[:], 1.0)
+        wos = const.tile([P, 2 * DOUT], U8, name="wos", align_bytes=64)
+        nc.vector.memset(wos[:].bitcast(I32), 0)
+        ident_f = const.tile([P, P], F32, name="ident_f")
+        make_identity(nc, ident_f[:])
+
+        w_bf = const.tile([P, H], BF16, name="w_bf")
+        b_bf = const.tile([P, H], BF16, name="b_bf")
+        d_bf = const.tile([P, H], BF16, name="d_bf")
+        with nc.allow_non_contiguous_dma(reason="two bf16 scalars of each small input, spread over the partitions"):
+            nc.scalar.dma_start(out=d_bf[:], in_=decay_values.partition_broadcast(P))
+            nc.scalar.dma_start(out=w_bf[:], in_=w_mix[:, index].partition_broadcast(P))
+            nc.scalar.dma_start(out=b_bf[:], in_=b_mix[:, index].partition_broadcast(P))
+        nc.scalar.activation(out=warm2[:], in_=warm[:], func=ACT.Sqrt)
+
+        ident_b = const.tile([P, P], BF16, name="ident_b")
+        nc.vector.tensor_copy(out=ident_b[:], in_=ident_f[:])
+        zrows = const.tile([P, NB], BF16, name="zrows")
+        nc.vector.tensor_copy(out=zrows[:], in_=ident_b[:, ONES_ROW : ONES_ROW + 1].to_broadcast([P, NB]))
+        nc.scalar.dma_start(out=zrows[0:8, :], in_=b_proj.rearrange("h (j n) -> (h j) n", n=NB))
+        nc.scalar.dma_start(out=zrows[8:12, :], in_=b_out.rearrange("(j n) -> j n", n=NB))
+
+        x_sb = act.tile([P, DIM], BF16, tag="rows", name="x_sb", align_bytes=64)
+        cch = const.tile([P, H, HID], BF16, name="cch")
+        raws = {}
+
+        def load(i):
+            if i == 4:
+                nc.sync.dma_start(out=cch[:, 0, :], in_=caches[0])
+            if i == 10:
+                nc.sync.dma_start(out=cch[:, 1, :], in_=caches[1])
+            if i == NCH:
+                for t in range(2):
+                    for q in range(4):
+                        nc.sync.dma_start(
+                            out=wos[32 * q : 32 * q + 16, DOUT * t : DOUT * (t + 1)].bitcast(I32),
+                            in_=W_out_scales[4 * t : 4 * t + 4, 4 * q : 4 * q + 4, :].bitcast(I32),
+                        )
+            if i < NCH:
+                h, kp = divmod(i, PASSES)
+                raw = ring.tile([P, PACK, HID], BF16, tag="ring", name="raw", align_bytes=64)
+                rows = W_proj[h, KP * kp : KP * (kp + 1), :]
+                if i == 0:
+                    nc.sync.dma_start(
+                        out=raw[:, :, 0:HALF], in_=rows[:, 0:HALF].rearrange("(p j) w -> p j w", j=PACK)
+                    )
+                    nc.sync.dma_start(out=x_sb[:], in_=x)
+                    nc.sync.dma_start(
+                        out=raw[:, :, HALF:HID], in_=rows[:, HALF:HID].rearrange("(p j) w -> p j w", j=PACK)
+                    )
+                else:
+                    nc.sync.dma_start(
+                        out=raw[:].rearrange("p j w -> p (j w)"), in_=rows.rearrange("(p j) w -> p (j w)", j=PACK)
+                    )
+                raws[i] = raw
+            else:
+                pr = i - NCH
+                wo = ring.tile([P, 2 * DOUT], U32, tag="ring", name="wo", align_bytes=64)
+                dst = wo[:].bitcast(I32).rearrange("p (g n) -> p g n", g=2)
+                words = W_out_words[2 * pr : 2 * pr + 2].rearrange("g p n t -> p g (n t)").bitcast(I32)
+                if pr < NPAIR - 1:
+                    nc.sync.dma_start(out=dst, in_=words)
+                else:
+                    for j in range(4):
+                        nc.sync.dma_start(out=dst[:, :, NB * j : NB * (j + 1)], in_=words[:, :, NB * j : NB * (j + 1)])
+                raws[i] = wo
+
+        for i in range(RING - 1):
+            load(i)
+
+        w_f = const.tile([P, H], F32, name="w_f")
+        b_f = const.tile([P, H], F32, name="b_f")
+        dcl = const.tile([P, H], F32, name="dcl")
+        rcp = const.tile([P, H], F32, name="rcp")
+        rt2 = const.tile([P, H], F32, name="rt2")
+        rt4 = const.tile([P, H], F32, name="rt4")
+        y2 = const.tile([P, H], F32, name="y2")
+        y4 = const.tile([P, H], F32, name="y4")
+        res = const.tile([P, H], F32, name="res")
+        cor = const.tile([P, H], F32, name="cor")
+        dec = const.tile([P, H], F32, name="dec")
+        coef = const.tile([P, H], F32, name="coef")
+        sel_f = const.tile([P, 8], F32, name="sel_f")
+        sel = const.tile([P, 8], BF16, name="sel")
+
+        def scalars_first():
+            nc.vector.tensor_scalar(out=dcl[:], in0=d_bf[:], scalar1=0.9, scalar2=1.0, op0=ALU.max, op1=ALU.min)
+            nc.scalar.activation(out=rt2[:], in_=dcl[:], func=ACT.Sqrt)
+            nc.scalar.activation(out=rt4[:], in_=rt2[:], func=ACT.Sqrt)
+            nc.vector.reciprocal(out=rcp[:], in_=dcl[:])
+            nc.vector.tensor_copy(out=w_f[:], in_=w_bf[:])
+            nc.vector.tensor_copy(out=b_f[:], in_=b_bf[:])
+
+        def scalars_second():
+            nc.vector.tensor_mul(out=y2[:], in0=rt4[:], in1=rt4[:])
+            nc.vector.tensor_mul(out=y4[:], in0=y2[:], in1=y2[:])
+            nc.vector.tensor_sub(out=res[:], in0=dcl[:], in1=y4[:])
+            nc.vector.tensor_mul(out=res[:], in0=res[:], in1=rcp[:])
+            nc.vector.tensor_mul(out=cor[:], in0=res[:], in1=rt4[:])
+            nc.vector.scalar_tensor_tensor(
+                out=dec[:], in0=cor[:], scalar=0.25, in1=rt4[:], op0=ALU.mult, op1=ALU.add
+            )
+            nc.vector.tensor_mul(out=coef[:, 0:1], in0=w_f[:, 0:1], in1=dec[:, 0:1])
+            nc.vector.tensor_copy(out=coef[:, 1:2], in_=dec[:, 1:2])
+            for h in range(H):
+                nc.vector.tensor_scalar(
+                    out=sel_f[:, 4 * h : 4 * h + 4], in0=ident_f[:, 4 * h : 4 * h + 4],
+                    scalar1=w_f[:, h : h + 1], scalar2=None, op0=ALU.mult,
+                )
+                nc.vector.scalar_tensor_tensor(
+                    out=sel[:, 4 * h : 4 * h + 4],
+                    in0=ident_f[:, ONES_ROW : ONES_ROW + 1].to_broadcast([P, 4]),
+                    scalar=b_f[:, h : h + 1], in1=sel_f[:, 4 * h : 4 * h + 4], op0=ALU.mult, op1=ALU.add,
+                )
+
+        xw = x_sb[:].bitcast(F32)
+        xg = act.tile([P, DIM], BF16, tag="grouped", name="xg", align_bytes=64)
+        xg_w = xg[:].bitcast(F32).rearrange("p (g b u) -> p g b u", g=PASSES, u=2)
+        xc = const.tile([P, PASSES * P], U32, name="xc", align_bytes=64)
+        xs = const.tile([P, PASSES * P], U8, name="xs", align_bytes=64)
+
+        def prepare_x():
+            for i in range(4):
+                xt = psum.tile([P, 2, 2, P], F32, tag="B%d" % i, name="xt")
+                for gg in range(2):
+                    g = 2 * i + gg
+                    for u in range(2):
+                        nc.tensor.transpose(xt[:, gg, u, :], xw[:, 256 * g + u : 256 * (g + 1) : 2], ident_f[:])
+                src = xt[:].rearrange("p g u b -> p g b u")
+                if i % 2 == 0:
+                    nc.vector.tensor_copy(out=xg_w[:, 2 * i : 2 * i + 2, :, :], in_=src)
+                else:
+                    nc.scalar.copy(out=xg_w[:, 2 * i : 2 * i + 2, :, :], in_=src)
+            for i in range(2):
+                nc.vector.quantize_mx(
+                    out=xc[:, 512 * i : 512 * (i + 1)].bitcast(FP8X4),
+                    scales=xs[:, 512 * i : 512 * (i + 1)],
+                    in_=xg[:, 2048 * i : 2048 * (i + 1)],
+                )
+
+        bout = const.tile([P, DOUT], BF16, name="bout")
+
+        def spread_rows(picks, first, bank):
+            blocks = []
+            for j in range(4):
+                bps = psum.tile([P, NB], F32, tag="%s%d" % (bank, j), name="bps")
+                nc.tensor.matmul(
+                    out=bps[:], lhsT=picks[:, first + j : first + j + 1].to_broadcast([P, P]), rhs=zrows[:],
+                    start=True, stop=True,
+                )
+                blocks.append(bps)
+            return blocks
+
+        def make_t(h, blocks):
+            t_h = tpool.tile([P, HID], F32, tag="wide", name="t_h")
+            for j in range(4):
+                nc.vector.scalar_tensor_tensor(
+                    out=t_h[:, NB * j : NB * (j + 1)], in0=cch[:, h, NB * j : NB * (j + 1)],
+                    scalar=coef[:, h : h + 1], in1=blocks[j][:], op0=ALU.mult, op1=ALU.add,
+                )
+            return t_h
+
+        acc = {}
+
+        def open_banks(h, bank):
+            for j in range(4):
+                a = psum.tile([P, NB], F32, tag="%s%d" % (bank, j), name="acc1")
+                acc[(h, j)] = a
+
+        def regroup(c, q, on_vector):
+            g_t = grp.tile([P, NB, PACK], BF16, tag="g_t", name="g_t", align_bytes=64)
+            src = raws[c][:, :, NB * q : NB * (q + 1)].rearrange("p t (c i) -> p c t i", i=4)
+            dst = g_t[:].rearrange("p (c i) t -> p c t i", i=4)
+            if on_vector:
+                nc.vector.tensor_copy(out=dst, in_=src)
+            else:
+                nc.scalar.copy(out=dst, in_=src)
+            return g_t
+
+        def quantise_and_multiply(c, q, g_t):
+            h, kp = divmod(c, PASSES)
+            wc = cod.tile([P, NB], U32, tag="wc", name="wc", align_bytes=64)
+            ws = cod.tile([P, NB], U8, tag="ws", name="ws", align_bytes=64)
+            nc.vector.quantize_mx(
+                out=wc[:].bitcast(FP8X4), scales=ws[:], in_=g_t[:].rearrange("p c t -> p (c t)")
+            )
+            nc.tensor.matmul_mx(
+                out=acc[(h, q)][:],
+                lhsT=xc[:, P * kp : P * (kp + 1)].bitcast(FP8X4),
+                lhsT_scale=xs[:, P * kp : P * (kp + 1)],
+                rhs=wc[:].bitcast(FP8X4),
+                rhs_scale=ws[:],
+                start=(kp == 0),
+                stop=(kp == PASSES - 1),
+            )
+
+        hidden = {}
+
+        def allocate_hidden():
+            hid = act.tile([P, H * HID], BF16, tag="rows", name="hid", align_bytes=64)
+            hg = act.tile([P, H * HID], BF16, tag="grouped", name="hg", align_bytes=64)
+            hidden["rows"] = hid
+            hidden["words"] = hid[:].bitcast(F32)
+            hidden["grouped"] = hg
+            hidden["grouped_words"] = hg[:].bitcast(F32).rearrange("p (g b u) -> p g b u", g=8, u=2)
+
+        hc = const.tile([P, 8 * P], U32, name="hc", align_bytes=64)
+        hs = const.tile([P, 8 * P], U8, name="hs", align_bytes=64)
+        t_of = {}
+        turned = {}
+
+        def mix(g):
+            h, j = divmod(g, 4)
+            nc.vector.scalar_tensor_tensor(
+                out=hidden["rows"][:, NB * g : NB * (g + 1)], in0=acc[(h, j)][:],
+                scalar=w_f[:, h : h + 1], in1=t_of[h][:, NB * j : NB * (j + 1)], op0=ALU.mult, op1=ALU.add,
+            )
+
+        def turn(g, bank):
+            ht = psum.tile([P, 2, P], F32, tag="%s%d" % (bank, g % 4), name="ht")
+            for u in range(2):
+                nc.tensor.transpose(ht[:, u, :], hidden["words"][:, 256 * g + u : 256 * (g + 1) : 2], ident_f[:])
+            turned[g] = ht
+
+        def collect(g):
+            nc.scalar.copy(out=hidden["grouped_words"][:, g, :, :], in_=turned[g][:].rearrange("p u b -> p b u"))
+
+        def quantise_hidden(g, n):
+            nc.vector.quantize_mx(
+                out=hc[:, P * g : P * (g + n)].bitcast(FP8X4), scales=hs[:, P * g : P * (g + n)],
+                in_=hidden["grouped"][:, KP * g : KP * (g + n)],
+            )
+
+        acc2 = []
+
+        def stage2_pass(g, j):
+            wo = raws[NCH + g // 2]
+            k = 4 * (g % 4)
+            col = DOUT * (g % 2) + NB * j
+            pcol = DOUT * (g // 4) + NB * j
+            nc.tensor.matmul_mx(
+                out=acc2[j][:],
+                lhsT=hc[:, P * g : P * (g + 1)].bitcast(FP8X4),
+                lhsT_scale=hs[:, P * g : P * (g + 1)],
+                rhs=wo[:, col : col + NB].bitcast(FP8X4),
+                rhs_scale=wos[k:P, pcol : pcol + NB],
+                start=(g == 0),
+                stop=(g == 7),
+            )
+
+        early_groups = {(14, 0): 0, (14, 1): 1, (15, 0): 2, (15, 1): 3}
+        open_banks(0, "A")
+        blocks = {}
+        left = None
+        for c in range(NCH):
+            if c + RING - 1 < NCH + NPAIR:
+                load(c + RING - 1)
+            if c == PASSES:
+                open_banks(1, "B")
+            g_of = {}
+            if c == 0:
+                g_of[1] = regroup(0, 1, False)
+                g_of[0] = regroup(0, 0, True)
+                scalars_first()
+                prepare_x()
+                scalars_second()
+                g_of[3] = regroup(0, 3, False)
+                g_of[2] = regroup(0, 2, True)
+            else:
+                on_vector = (0,) if c in V_LIGHT else (0, 2)
+                for q in range(4):
+                    if q not in on_vector:
+                        g_of[q] = regroup(c, q, False)
+                g_of[0] = regroup(c, 0, True)
+                quantise_and_multiply(c - 1, 3, left)
+                if c == PASSES:
+                    for g in range(4):
+                        mix(g)
+                if 2 in on_vector:
+                    g_of[2] = regroup(c, 2, True)
+            if c == 5:
+                t_of[0] = make_t(0, blocks[0])
+            if c == 12:
+                t_of[1] = make_t(1, blocks[1])
+            for q in range(3):
+                quantise_and_multiply(c, q, g_of[q])
+                if (c, q) in early_groups:
+                    for j in range(4):
+                        stage2_pass(early_groups[(c, q)], j)
+            left = g_of[3]
+            if c == 1:
+                allocate_hidden()
+                blocks[0] = spread_rows(sel, 0, "B")
+            if c == 9:
+                for g in range(4):
+                    turn(g, "A")
+            if c == 10:
+                for g in range(4):
+                    collect(g)
+            if c == 11:
+                quantise_hidden(0, 4)
+                blocks[1] = spread_rows(sel, 4, "A")
+            if c == 13:
+                blocks[2] = spread_rows(ident_b, 8, "A")
+                for j in range(4):
+                    nc.scalar.copy(out=bout[:, NB * j : NB * (j + 1)], in_=blocks[2][j][:])
+                for j in range(4):
+                    a2 = psum.tile([P, NB], F32, tag="A%d" % j, name="acc2")
+                    acc2.append(a2)
+
+        mix(4)
+        mix(5)
+        turn(4, "B")
+        turn(5, "B")
+        collect(4)
+        collect(5)
+        quantise_and_multiply(NCH - 1, 3, left)
+        mix(6)
+        quantise_hidden(4, 1)
+        quantise_hidden(5, 1)
+        turn(6, "B")
+        collect(6)
+        for j in range(4):
+            stage2_pass(4, j)
+        mix(7)
+        turn(7, "B")
+        collect(7)
+        quantise_hidden(6, 1)
+        quantise_hidden(7, 1)
+        for j in range(4):
+            stage2_pass(5, j)
+        o_sb = tpool.tile([P, DOUT], F32, tag="wide", name="o_sb")
+        for j in range(4):
+            stage2_pass(6, j)
+            stage2_pass(7, j)
+            nc.vector.tensor_tensor(
+                out=o_sb[:, NB * j : NB * (j + 1)], in0=acc2[j][:], in1=bout[:, NB * j : NB * (j + 1)], op=ALU.add
+            )
+            nc.sync.dma_start(out=out[:, NB * j : NB * (j + 1)], in_=o_sb[:, NB * j : NB * (j + 1)])

@@ -35,8 +35,8 @@ def tile_mixedrepeatheads_w_kernel(
     with ExitStack() as ctx:
         const = ctx.enter_context(tc.tile_pool(name="const", bufs=1))
         ring = ctx.enter_context(tc.tile_pool(name="ring", bufs=RING))
-        grp = ctx.enter_context(tc.tile_pool(name="grp", bufs=8))
-        cod = ctx.enter_context(tc.tile_pool(name="cod", bufs=6))
+        grp = ctx.enter_context(tc.tile_pool(name="grp", bufs=4))
+        cod = ctx.enter_context(tc.tile_pool(name="cod", bufs=4))
         act = ctx.enter_context(tc.tile_pool(name="act", bufs=1))
         tpool = ctx.enter_context(tc.tile_pool(name="tpool", bufs=2))
         psum = ctx.enter_context(tc.psum_pool(name="psum", bufs=1))
@@ -213,32 +213,35 @@ def tile_mixedrepeatheads_w_kernel(
                 a = psum.tile([P, NB], F32, tag="%s%d" % (bank, j), name="acc1")
                 acc[(h, j)] = a
 
-        def regroup(c, q, on_vector):
-            g_t = grp.tile([P, NB, PACK], BF16, tag="g_t", name="g_t", align_bytes=64)
+        def new_half():
+            g_t = grp.tile([P, HALF, PACK], BF16, tag="g_t", name="g_t", align_bytes=64)
+            return g_t
+
+        def regroup(c, q, on_vector, g_t):
             src = raws[c][:, :, NB * q : NB * (q + 1)].rearrange("p t (c i) -> p c t i", i=4)
-            dst = g_t[:].rearrange("p (c i) t -> p c t i", i=4)
+            dst = g_t[:, NB * (q % 2) : NB * (q % 2 + 1), :].rearrange("p (c i) t -> p c t i", i=4)
             if on_vector:
                 nc.vector.tensor_copy(out=dst, in_=src)
             else:
                 nc.scalar.copy(out=dst, in_=src)
-            return g_t
 
-        def quantise_and_multiply(c, q, g_t):
+        def quantise_and_multiply(c, hf, g_t):
             h, kp = divmod(c, PASSES)
-            wc = cod.tile([P, NB], U32, tag="wc", name="wc", align_bytes=64)
-            ws = cod.tile([P, NB], U8, tag="ws", name="ws", align_bytes=64)
+            wc = cod.tile([P, HALF], U32, tag="wc", name="wc", align_bytes=64)
+            ws = cod.tile([P, HALF], U8, tag="ws", name="ws", align_bytes=64)
             nc.vector.quantize_mx(
                 out=wc[:].bitcast(FP8X4), scales=ws[:], in_=g_t[:].rearrange("p c t -> p (c t)")
             )
-            nc.tensor.matmul_mx(
-                out=acc[(h, q)][:],
-                lhsT=xc[:, P * kp : P * (kp + 1)].bitcast(FP8X4),
-                lhsT_scale=xs[:, P * kp : P * (kp + 1)],
-                rhs=wc[:].bitcast(FP8X4),
-                rhs_scale=ws[:],
-                start=(kp == 0),
-                stop=(kp == PASSES - 1),
-            )
+            for jj in range(2):
+                nc.tensor.matmul_mx(
+                    out=acc[(h, 2 * hf + jj)][:],
+                    lhsT=xc[:, P * kp : P * (kp + 1)].bitcast(FP8X4),
+                    lhsT_scale=xs[:, P * kp : P * (kp + 1)],
+                    rhs=wc[:, NB * jj : NB * (jj + 1)].bitcast(FP8X4),
+                    rhs_scale=ws[:, NB * jj : NB * (jj + 1)],
+                    start=(kp == 0),
+                    stop=(kp == PASSES - 1),
+                )
 
         hidden = {}
 
@@ -295,6 +298,12 @@ def tile_mixedrepeatheads_w_kernel(
             )
 
         early_groups = {(14, 0): 0, (14, 1): 1, (15, 0): 2, (15, 1): 3}
+
+        def early(c, slot):
+            if (c, slot) in early_groups:
+                for j in range(4):
+                    stage2_pass(early_groups[(c, slot)], j)
+
         open_banks(0, "A")
         blocks = {}
         left = None
@@ -303,39 +312,41 @@ def tile_mixedrepeatheads_w_kernel(
                 load(c + RING - 1)
             if c == PASSES:
                 open_banks(1, "B")
-            g_of = {}
+            h0 = new_half()
+            h1 = new_half()
             if c == 0:
-                g_of[1] = regroup(0, 1, False)
-                g_of[0] = regroup(0, 0, True)
-                scalars_first()
+                regroup(0, 1, False, h0)
+                regroup(0, 0, True, h0)
                 prepare_x()
-                scalars_second()
-                g_of[3] = regroup(0, 3, False)
-                g_of[2] = regroup(0, 2, True)
+                regroup(0, 3, False, h1)
+                regroup(0, 2, True, h1)
             else:
-                on_vector = (0,) if c in V_LIGHT else (0, 2)
-                for q in range(4):
-                    if q not in on_vector:
-                        g_of[q] = regroup(c, q, False)
-                g_of[0] = regroup(c, 0, True)
-                quantise_and_multiply(c - 1, 3, left)
+                light = c in V_LIGHT
+                regroup(c, 1, False, h0)
+                if light:
+                    regroup(c, 2, False, h1)
+                regroup(c, 3, False, h1)
+                regroup(c, 0, True, h0)
+                quantise_and_multiply(c - 1, 1, left)
+                early(c, 0)
                 if c == PASSES:
                     for g in range(4):
                         mix(g)
-                if 2 in on_vector:
-                    g_of[2] = regroup(c, 2, True)
+                if not light:
+                    regroup(c, 2, True, h1)
             if c == 5:
                 t_of[0] = make_t(0, blocks[0])
             if c == 12:
                 t_of[1] = make_t(1, blocks[1])
-            for q in range(3):
-                quantise_and_multiply(c, q, g_of[q])
-                if (c, q) in early_groups:
-                    for j in range(4):
-                        stage2_pass(early_groups[(c, q)], j)
-            left = g_of[3]
+            quantise_and_multiply(c, 0, h0)
+            early(c, 1)
+            left = h1
             if c == 1:
                 allocate_hidden()
+                scalars_first()
+            if c == 2:
+                scalars_second()
+            if c == 3:
                 blocks[0] = spread_rows(sel, 0, "B")
             if c == 9:
                 for g in range(4):
@@ -360,14 +371,14 @@ def tile_mixedrepeatheads_w_kernel(
         turn(5, "B")
         collect(4)
         collect(5)
-        quantise_and_multiply(NCH - 1, 3, left)
-        mix(6)
+        quantise_and_multiply(NCH - 1, 1, left)
         quantise_hidden(4, 1)
         quantise_hidden(5, 1)
-        turn(6, "B")
-        collect(6)
+        mix(6)
         for j in range(4):
             stage2_pass(4, j)
+        turn(6, "B")
+        collect(6)
         mix(7)
         turn(7, "B")
         collect(7)

@@ -22,7 +22,7 @@ NCH = H * PASSES
 HALF = HID // 2
 RING = 7
 NPAIR = 4
-V_LIGHT = (5, 8, 12)
+V_LIGHT = (1, 8)
 ONES_ROW = 32
 
 FLOPS = 2 * B * DIM * H * HID + 2 * B * H * HID * DOUT
@@ -71,10 +71,9 @@ def tile_mixedrepeatheads_w_kernel(
         raws = {}
 
         def load(i):
-            if i == 4:
-                nc.sync.dma_start(out=cch[:, 0, :], in_=caches[0])
-            if i == 10:
-                nc.sync.dma_start(out=cch[:, 1, :], in_=caches[1])
+            if i == 1:
+                nc.sync.dma_start(out=cch[:], in_=caches.rearrange("h b n -> b h n"))
+                nc.sync.dma_start(out=x_sb[:], in_=x)
             if i == NCH:
                 for t in range(2):
                     for q in range(4):
@@ -82,33 +81,32 @@ def tile_mixedrepeatheads_w_kernel(
                             out=wos[32 * q : 32 * q + 16, DOUT * t : DOUT * (t + 1)].bitcast(I32),
                             in_=W_out_scales[4 * t : 4 * t + 4, 4 * q : 4 * q + 4, :].bitcast(I32),
                         )
-            if i < NCH:
+            if i == 0:
+                raw = ring.tile([P, 2, PACK, HALF], BF16, tag="ring", name="raw0", align_bytes=64)
+                for hf in range(2):
+                    nc.sync.dma_start(
+                        out=raw[:, hf, :, :],
+                        in_=W_proj[0, 0:KP, HALF * hf : HALF * (hf + 1)].rearrange("(p j) w -> p j w", j=PACK),
+                    )
+                raws[i] = raw
+            elif i < NCH:
                 h, kp = divmod(i, PASSES)
                 raw = ring.tile([P, PACK, HID], BF16, tag="ring", name="raw", align_bytes=64)
-                rows = W_proj[h, KP * kp : KP * (kp + 1), :]
-                if i == 0:
-                    nc.sync.dma_start(
-                        out=raw[:, :, 0:HALF], in_=rows[:, 0:HALF].rearrange("(p j) w -> p j w", j=PACK)
-                    )
-                    nc.sync.dma_start(out=x_sb[:], in_=x)
-                    nc.sync.dma_start(
-                        out=raw[:, :, HALF:HID], in_=rows[:, HALF:HID].rearrange("(p j) w -> p j w", j=PACK)
-                    )
-                else:
-                    nc.sync.dma_start(
-                        out=raw[:].rearrange("p j w -> p (j w)"), in_=rows.rearrange("(p j) w -> p (j w)", j=PACK)
-                    )
+                nc.sync.dma_start(
+                    out=raw[:].rearrange("p j w -> p (j w)"),
+                    in_=W_proj[h, KP * kp : KP * (kp + 1), :].rearrange("(p j) w -> p (j w)", j=PACK),
+                )
                 raws[i] = raw
             else:
                 pr = i - NCH
                 wo = ring.tile([P, 2 * DOUT], U32, tag="ring", name="wo", align_bytes=64)
-                dst = wo[:].bitcast(I32).rearrange("p (g n) -> p g n", g=2)
                 words = W_out_words[2 * pr : 2 * pr + 2].rearrange("g p n t -> p g (n t)").bitcast(I32)
                 if pr < NPAIR - 1:
-                    nc.sync.dma_start(out=dst, in_=words)
+                    nc.sync.dma_start(out=wo[:].bitcast(I32).rearrange("p (g n) -> p g n", g=2), in_=words)
                 else:
+                    dst = wo[:].bitcast(I32).rearrange("p (j g n) -> p j g n", j=4, g=2)
                     for j in range(4):
-                        nc.sync.dma_start(out=dst[:, :, NB * j : NB * (j + 1)], in_=words[:, :, NB * j : NB * (j + 1)])
+                        nc.sync.dma_start(out=dst[:, j, :, :], in_=words[:, :, NB * j : NB * (j + 1)])
                 raws[i] = wo
 
         for i in range(RING - 1):
@@ -218,20 +216,28 @@ def tile_mixedrepeatheads_w_kernel(
             return g_t
 
         def regroup(c, q, on_vector, g_t):
-            src = raws[c][:, :, NB * q : NB * (q + 1)].rearrange("p t (c i) -> p c t i", i=4)
+            if c == 0:
+                part = raws[0][:, q // 2, :, NB * (q % 2) : NB * (q % 2 + 1)]
+            else:
+                part = raws[c][:, :, NB * q : NB * (q + 1)]
+            src = part.rearrange("p t (c i) -> p c t i", i=4)
             dst = g_t[:, NB * (q % 2) : NB * (q % 2 + 1), :].rearrange("p (c i) t -> p c t i", i=4)
             if on_vector:
                 nc.vector.tensor_copy(out=dst, in_=src)
             else:
                 nc.scalar.copy(out=dst, in_=src)
 
-        def quantise_and_multiply(c, hf, g_t):
-            h, kp = divmod(c, PASSES)
+        def quantise(g_t):
             wc = cod.tile([P, HALF], U32, tag="wc", name="wc", align_bytes=64)
             ws = cod.tile([P, HALF], U8, tag="ws", name="ws", align_bytes=64)
             nc.vector.quantize_mx(
                 out=wc[:].bitcast(FP8X4), scales=ws[:], in_=g_t[:].rearrange("p c t -> p (c t)")
             )
+            return wc, ws
+
+        def multiply(c, hf, codes):
+            h, kp = divmod(c, PASSES)
+            wc, ws = codes
             for jj in range(2):
                 nc.tensor.matmul_mx(
                     out=acc[(h, 2 * hf + jj)][:],
@@ -242,6 +248,9 @@ def tile_mixedrepeatheads_w_kernel(
                     start=(kp == 0),
                     stop=(kp == PASSES - 1),
                 )
+
+        def quantise_and_multiply(c, hf, g_t):
+            multiply(c, hf, quantise(g_t))
 
         hidden = {}
 
@@ -285,7 +294,10 @@ def tile_mixedrepeatheads_w_kernel(
         def stage2_pass(g, j):
             wo = raws[NCH + g // 2]
             k = 4 * (g % 4)
-            col = DOUT * (g % 2) + NB * j
+            if g < 6:
+                col = DOUT * (g % 2) + NB * j
+            else:
+                col = NB * (2 * j + g % 2)
             pcol = DOUT * (g // 4) + NB * j
             nc.tensor.matmul_mx(
                 out=acc2[j][:],
@@ -304,7 +316,6 @@ def tile_mixedrepeatheads_w_kernel(
                 for j in range(4):
                     stage2_pass(early_groups[(c, slot)], j)
 
-        open_banks(0, "A")
         blocks = {}
         left = None
         for c in range(NCH):
@@ -315,39 +326,44 @@ def tile_mixedrepeatheads_w_kernel(
             h0 = new_half()
             h1 = new_half()
             if c == 0:
+                blocks[2] = spread_rows(ident_b, 8, "A")
                 regroup(0, 1, False, h0)
                 regroup(0, 0, True, h0)
-                prepare_x()
+                scalars_first()
                 regroup(0, 3, False, h1)
                 regroup(0, 2, True, h1)
-            else:
-                light = c in V_LIGHT
-                regroup(c, 1, False, h0)
-                if light:
-                    regroup(c, 2, False, h1)
-                regroup(c, 3, False, h1)
-                regroup(c, 0, True, h0)
-                quantise_and_multiply(c - 1, 1, left)
-                early(c, 0)
-                if c == PASSES:
-                    for g in range(4):
-                        mix(g)
-                if not light:
-                    regroup(c, 2, True, h1)
-            if c == 5:
+                codes0 = quantise(h0)
+                scalars_second()
+                for j in range(4):
+                    nc.scalar.copy(out=bout[:, NB * j : NB * (j + 1)], in_=blocks[2][j][:])
+                blocks[0] = spread_rows(sel, 0, "B")
+                codes1 = quantise(h1)
                 t_of[0] = make_t(0, blocks[0])
-            if c == 12:
+                blocks[1] = spread_rows(sel, 4, "A")
                 t_of[1] = make_t(1, blocks[1])
+                prepare_x()
+                open_banks(0, "A")
+                multiply(0, 0, codes0)
+                multiply(0, 1, codes1)
+                allocate_hidden()
+                continue
+            light = c in V_LIGHT
+            regroup(c, 1, False, h0)
+            if light:
+                regroup(c, 2, False, h1)
+            regroup(c, 3, False, h1)
+            regroup(c, 0, True, h0)
+            if left is not None:
+                quantise_and_multiply(c - 1, 1, left)
+            early(c, 0)
+            if c == PASSES:
+                for g in range(4):
+                    mix(g)
+            if not light:
+                regroup(c, 2, True, h1)
             quantise_and_multiply(c, 0, h0)
             early(c, 1)
             left = h1
-            if c == 1:
-                allocate_hidden()
-                scalars_first()
-            if c == 2:
-                scalars_second()
-            if c == 3:
-                blocks[0] = spread_rows(sel, 0, "B")
             if c == 9:
                 for g in range(4):
                     turn(g, "A")
@@ -356,11 +372,7 @@ def tile_mixedrepeatheads_w_kernel(
                     collect(g)
             if c == 11:
                 quantise_hidden(0, 4)
-                blocks[1] = spread_rows(sel, 4, "A")
-            if c == 13:
-                blocks[2] = spread_rows(ident_b, 8, "A")
-                for j in range(4):
-                    nc.scalar.copy(out=bout[:, NB * j : NB * (j + 1)], in_=blocks[2][j][:])
+            if c == 12:
                 for j in range(4):
                     a2 = psum.tile([P, NB], F32, tag="A%d" % j, name="acc2")
                     acc2.append(a2)

@@ -22,7 +22,7 @@ NCH = H * PASSES
 HALF = HID // 2
 RING = 7
 NPAIR = 4
-V_LIGHT = (1, 8)
+V_LIGHT = (8, 14)
 ONES_ROW = 32
 
 FLOPS = 2 * B * DIM * H * HID + 2 * B * H * HID * DOUT
@@ -42,6 +42,11 @@ def tile_mixedrepeatheads_w_kernel(
         psum = ctx.enter_context(tc.psum_pool(name="psum", bufs=1))
         ctx.enter_context(tc.manual_schedule())
 
+        zrows = const.tile([P, NB], BF16, name="zrows")
+        nc.vector.memset(zrows[:].bitcast(I32), 0)
+        nc.vector.memset(zrows[ONES_ROW : ONES_ROW + 1, :], 1.0)
+        nc.sync.dma_start(out=zrows[0:8, :], in_=b_proj.rearrange("h (j n) -> (h j) n", n=NB))
+        nc.sync.dma_start(out=zrows[8:12, :], in_=b_out.rearrange("(j n) -> j n", n=NB))
         warm = const.tile([P, 1], F32, name="warm")
         warm2 = const.tile([P, 1], F32, name="warm2")
         nc.vector.memset(warm[:], 1.0)
@@ -61,10 +66,6 @@ def tile_mixedrepeatheads_w_kernel(
 
         ident_b = const.tile([P, P], BF16, name="ident_b")
         nc.vector.tensor_copy(out=ident_b[:], in_=ident_f[:])
-        zrows = const.tile([P, NB], BF16, name="zrows")
-        nc.vector.tensor_copy(out=zrows[:], in_=ident_b[:, ONES_ROW : ONES_ROW + 1].to_broadcast([P, NB]))
-        nc.scalar.dma_start(out=zrows[0:8, :], in_=b_proj.rearrange("h (j n) -> (h j) n", n=NB))
-        nc.scalar.dma_start(out=zrows[8:12, :], in_=b_out.rearrange("(j n) -> j n", n=NB))
 
         x_sb = act.tile([P, DIM], BF16, tag="rows", name="x_sb", align_bytes=64)
         cch = const.tile([P, H, HID], BF16, name="cch")
@@ -171,10 +172,7 @@ def tile_mixedrepeatheads_w_kernel(
                     for u in range(2):
                         nc.tensor.transpose(xt[:, gg, u, :], xw[:, 256 * g + u : 256 * (g + 1) : 2], ident_f[:])
                 src = xt[:].rearrange("p g u b -> p g b u")
-                if i % 2 == 0:
-                    nc.vector.tensor_copy(out=xg_w[:, 2 * i : 2 * i + 2, :, :], in_=src)
-                else:
-                    nc.scalar.copy(out=xg_w[:, 2 * i : 2 * i + 2, :, :], in_=src)
+                nc.scalar.copy(out=xg_w[:, 2 * i : 2 * i + 2, :, :], in_=src)
             for i in range(2):
                 nc.vector.quantize_mx(
                     out=xc[:, 512 * i : 512 * (i + 1)].bitcast(FP8X4),

@@ -54,6 +54,12 @@ def tile_mixedrepeatheads_w_kernel(
         nc.vector.memset(wos[:].bitcast(I32), 0)
         ident_f = const.tile([P, P], F32, name="ident_f")
         make_identity(nc, ident_f[:])
+        for t in range(2):
+            for q in range(4):
+                nc.gpsimd.dma_start(
+                    out=wos[32 * q : 32 * q + 16, DOUT * t : DOUT * (t + 1)].bitcast(F32),
+                    in_=W_out_scales[4 * t : 4 * t + 4, 4 * q : 4 * q + 4, :].bitcast(F32),
+                )
 
         w_bf = const.tile([P, H], BF16, name="w_bf")
         b_bf = const.tile([P, H], BF16, name="b_bf")
@@ -75,13 +81,6 @@ def tile_mixedrepeatheads_w_kernel(
             if i == 1:
                 nc.sync.dma_start(out=cch[:], in_=caches.rearrange("h b n -> b h n"))
                 nc.sync.dma_start(out=x_sb[:], in_=x)
-            if i == NCH:
-                for t in range(2):
-                    for q in range(4):
-                        nc.sync.dma_start(
-                            out=wos[32 * q : 32 * q + 16, DOUT * t : DOUT * (t + 1)].bitcast(I32),
-                            in_=W_out_scales[4 * t : 4 * t + 4, 4 * q : 4 * q + 4, :].bitcast(I32),
-                        )
             if i == 0:
                 raw = ring.tile([P, 2, PACK, HALF], BF16, tag="ring", name="raw0", align_bytes=64)
                 for hf in range(2):

@@ -22,7 +22,7 @@ NCH = H * PASSES
 HALF = HID // 2
 RING = 7
 NPAIR = 4
-V_LIGHT = (8, 14)
+V_LIGHT = ()
 ONES_ROW = 32
 
 FLOPS = 2 * B * DIM * H * HID + 2 * B * H * HID * DOUT

@@ -356,10 +356,12 @@ def tile_mixedrepeatheads_w_kernel(
             if c == PASSES:
                 for g in range(4):
                     mix(g)
-            if not light:
+            if not light and c < NCH - 1:
                 regroup(c, 2, True, h1)
             quantise_and_multiply(c, 0, h0)
             early(c, 1)
+            if c == NCH - 1:
+                regroup(c, 2, True, h1)
             left = h1
             if c == 9:
                 for g in range(4):

from contextlib import ExitStack

import concourse.mybir as mybir
from concourse.masks import make_identity

FP8X4 = mybir.dt.float8_e4m3fn_x4
BF16 = mybir.dt.bfloat16
F32 = mybir.dt.float32
I32 = mybir.dt.int32
U32 = mybir.dt.uint32
U8 = mybir.dt.uint8
ALU = mybir.AluOpType
ACT = mybir.ActivationFunctionType

P = 128
PACK = 4
KP = P * PACK
B, DIM, HID, H, DOUT = 128, 4096, 2048, 2, 2048
NB = 512
PASSES = DIM // KP
NCH = H * PASSES
HALF = HID // 2
RING = 7
NPAIR = 4
V_LIGHT = ()
ONES_ROW = 32

FLOPS = 2 * B * DIM * H * HID + 2 * B * H * HID * DOUT


def tile_mixedrepeatheads_w_kernel(
    tc, x, index, W_proj, b_proj, W_out_words, W_out_scales, b_out, w_mix, b_mix, decay_values, caches, out
):
    nc = tc.nc
    with ExitStack() as ctx:
        const = ctx.enter_context(tc.tile_pool(name="const", bufs=1))
        ring = ctx.enter_context(tc.tile_pool(name="ring", bufs=RING))
        grp = ctx.enter_context(tc.tile_pool(name="grp", bufs=4))
        cod = ctx.enter_context(tc.tile_pool(name="cod", bufs=4))
        act = ctx.enter_context(tc.tile_pool(name="act", bufs=1))
        tpool = ctx.enter_context(tc.tile_pool(name="tpool", bufs=2))
        psum = ctx.enter_context(tc.psum_pool(name="psum", bufs=1))
        ctx.enter_context(tc.manual_schedule())

        zrows = const.tile([P, NB], BF16, name="zrows")
        nc.vector.memset(zrows[:].bitcast(I32), 0)
        nc.vector.memset(zrows[ONES_ROW : ONES_ROW + 1, :], 1.0)
        nc.sync.dma_start(out=zrows[0:8, :], in_=b_proj.rearrange("h (j n) -> (h j) n", n=NB))
        nc.sync.dma_start(out=zrows[8:12, :], in_=b_out.rearrange("(j n) -> j n", n=NB))
        warm = const.tile([P, 1], F32, name="warm")
        warm2 = const.tile([P, 1], F32, name="warm2")
        nc.vector.memset(warm[:], 1.0)
        wos = const.tile([P, 2 * DOUT], U8, name="wos", align_bytes=64)
        nc.vector.memset(wos[:].bitcast(I32), 0)
        ident_f = const.tile([P, P], F32, name="ident_f")
        make_identity(nc, ident_f[:])
        for t in range(2):
            for q in range(4):
                nc.gpsimd.dma_start(
                    out=wos[32 * q : 32 * q + 16, DOUT * t : DOUT * (t + 1)].bitcast(F32),
                    in_=W_out_scales[4 * t : 4 * t + 4, 4 * q : 4 * q + 4, :].bitcast(F32),
                )

        w_bf = const.tile([P, H], BF16, name="w_bf")
        b_bf = const.tile([P, H], BF16, name="b_bf")
        d_bf = const.tile([P, H], BF16, name="d_bf")
        with nc.allow_non_contiguous_dma(reason="two bf16 scalars of each small input, spread over the partitions"):
            nc.scalar.dma_start(out=d_bf[:], in_=decay_values.partition_broadcast(P))
            nc.scalar.dma_start(out=w_bf[:], in_=w_mix[:, index].partition_broadcast(P))
            nc.scalar.dma_start(out=b_bf[:], in_=b_mix[:, index].partition_broadcast(P))
        nc.scalar.activation(out=warm2[:], in_=warm[:], func=ACT.Sqrt)

        ident_b = const.tile([P, P], BF16, name="ident_b")
        nc.vector.tensor_copy(out=ident_b[:], in_=ident_f[:])

        x_sb = act.tile([P, DIM], BF16, tag="rows", name="x_sb", align_bytes=64)
        cch = const.tile([P, H, HID], BF16, name="cch")
        raws = {}

        def load(i):
            if i == 1:
                nc.sync.dma_start(out=cch[:], in_=caches.rearrange("h b n -> b h n"))
                nc.sync.dma_start(out=x_sb[:], in_=x)
            if i == 0:
                raw = ring.tile([P, 2, PACK, HALF], BF16, tag="ring", name="raw0", align_bytes=64)
                for hf in range(2):
                    nc.sync.dma_start(
                        out=raw[:, hf, :, :],
                        in_=W_proj[0, 0:KP, HALF * hf : HALF * (hf + 1)].rearrange("(p j) w -> p j w", j=PACK),
                    )
                raws[i] = raw
            elif i < NCH:
                h, kp = divmod(i, PASSES)
                raw = ring.tile([P, PACK, HID], BF16, tag="ring", name="raw", align_bytes=64)
                nc.sync.dma_start(
                    out=raw[:].rearrange("p j w -> p (j w)"),
                    in_=W_proj[h, KP * kp : KP * (kp + 1), :].rearrange("(p j) w -> p (j w)", j=PACK),
                )
                raws[i] = raw
            else:
                pr = i - NCH
                wo = ring.tile([P, 2 * DOUT], U32, tag="ring", name="wo", align_bytes=64)
                words = W_out_words[2 * pr : 2 * pr + 2].rearrange("g p n t -> p g (n t)").bitcast(I32)
                if pr < NPAIR - 1:
                    nc.sync.dma_start(out=wo[:].bitcast(I32).rearrange("p (g n) -> p g n", g=2), in_=words)
                else:
                    dst = wo[:].bitcast(I32).rearrange("p (j g n) -> p j g n", j=4, g=2)
                    for j in range(4):
                        nc.sync.dma_start(out=dst[:, j, :, :], in_=words[:, :, NB * j : NB * (j + 1)])
                raws[i] = wo

        for i in range(RING - 1):
            load(i)

        w_f = const.tile([P, H], F32, name="w_f")
        b_f = const.tile([P, H], F32, name="b_f")
        dcl = const.tile([P, H], F32, name="dcl")
        rcp = const.tile([P, H], F32, name="rcp")
        rt2 = const.tile([P, H], F32, name="rt2")
        rt4 = const.tile([P, H], F32, name="rt4")
        y2 = const.tile([P, H], F32, name="y2")
        y4 = const.tile([P, H], F32, name="y4")
        res = const.tile([P, H], F32, name="res")
        cor = const.tile([P, H], F32, name="cor")
        dec = const.tile([P, H], F32, name="dec")
        coef = const.tile([P, H], F32, name="coef")
        sel_f = const.tile([P, 8], F32, name="sel_f")
        sel = const.tile([P, 8], BF16, name="sel")

        def scalars_first():
            nc.vector.tensor_scalar(out=dcl[:], in0=d_bf[:], scalar1=0.9, scalar2=1.0, op0=ALU.max, op1=ALU.min)
            nc.scalar.activation(out=rt2[:], in_=dcl[:], func=ACT.Sqrt)
            nc.scalar.activation(out=rt4[:], in_=rt2[:], func=ACT.Sqrt)
            nc.vector.reciprocal(out=rcp[:], in_=dcl[:])
            nc.vector.tensor_copy(out=w_f[:], in_=w_bf[:])
            nc.vector.tensor_copy(out=b_f[:], in_=b_bf[:])

        def scalars_second():
            nc.vector.tensor_mul(out=y2[:], in0=rt4[:], in1=rt4[:])
            nc.vector.tensor_mul(out=y4[:], in0=y2[:], in1=y2[:])
            nc.vector.tensor_sub(out=res[:], in0=dcl[:], in1=y4[:])
            nc.vector.tensor_mul(out=res[:], in0=res[:], in1=rcp[:])
            nc.vector.tensor_mul(out=cor[:], in0=res[:], in1=rt4[:])
            nc.vector.scalar_tensor_tensor(
                out=dec[:], in0=cor[:], scalar=0.25, in1=rt4[:], op0=ALU.mult, op1=ALU.add
            )
            nc.vector.tensor_mul(out=coef[:, 0:1], in0=w_f[:, 0:1], in1=dec[:, 0:1])
            nc.vector.tensor_copy(out=coef[:, 1:2], in_=dec[:, 1:2])
            for h in range(H):
                nc.vector.tensor_scalar(
                    out=sel_f[:, 4 * h : 4 * h + 4], in0=ident_f[:, 4 * h : 4 * h + 4],
                    scalar1=w_f[:, h : h + 1], scalar2=None, op0=ALU.mult,
                )
                nc.vector.scalar_tensor_tensor(
                    out=sel[:, 4 * h : 4 * h + 4],
                    in0=ident_f[:, ONES_ROW : ONES_ROW + 1].to_broadcast([P, 4]),
                    scalar=b_f[:, h : h + 1], in1=sel_f[:, 4 * h : 4 * h + 4], op0=ALU.mult, op1=ALU.add,
                )

        xw = x_sb[:].bitcast(F32)
        xg = act.tile([P, DIM], BF16, tag="grouped", name="xg", align_bytes=64)
        xg_w = xg[:].bitcast(F32).rearrange("p (g b u) -> p g b u", g=PASSES, u=2)
        xc = const.tile([P, PASSES * P], U32, name="xc", align_bytes=64)
        xs = const.tile([P, PASSES * P], U8, name="xs", align_bytes=64)

        def prepare_x():
            for i in range(4):
                xt = psum.tile([P, 2, 2, P], F32, tag="B%d" % i, name="xt")
                for gg in range(2):
                    g = 2 * i + gg
                    for u in range(2):
                        nc.tensor.transpose(xt[:, gg, u, :], xw[:, 256 * g + u : 256 * (g + 1) : 2], ident_f[:])
                src = xt[:].rearrange("p g u b -> p g b u")
                nc.scalar.copy(out=xg_w[:, 2 * i : 2 * i + 2, :, :], in_=src)
            for i in range(2):
                nc.vector.quantize_mx(
                    out=xc[:, 512 * i : 512 * (i + 1)].bitcast(FP8X4),
                    scales=xs[:, 512 * i : 512 * (i + 1)],
                    in_=xg[:, 2048 * i : 2048 * (i + 1)],
                )

        bout = const.tile([P, DOUT], BF16, name="bout")

        def spread_rows(picks, first, bank):
            blocks = []
            for j in range(4):
                bps = psum.tile([P, NB], F32, tag="%s%d" % (bank, j), name="bps")
                nc.tensor.matmul(
                    out=bps[:], lhsT=picks[:, first + j : first + j + 1].to_broadcast([P, P]), rhs=zrows[:],
                    start=True, stop=True,
                )
                blocks.append(bps)
            return blocks

        def make_t(h, blocks):
            t_h = tpool.tile([P, HID], F32, tag="wide", name="t_h")
            for j in range(4):
                nc.vector.scalar_tensor_tensor(
                    out=t_h[:, NB * j : NB * (j + 1)], in0=cch[:, h, NB * j : NB * (j + 1)],
                    scalar=coef[:, h : h + 1], in1=blocks[j][:], op0=ALU.mult, op1=ALU.add,
                )
            return t_h

        acc = {}

        def open_banks(h, bank):
            for j in range(4):
                a = psum.tile([P, NB], F32, tag="%s%d" % (bank, j), name="acc1")
                acc[(h, j)] = a

        def new_half():
            g_t = grp.tile([P, HALF, PACK], BF16, tag="g_t", name="g_t", align_bytes=64)
            return g_t

        def regroup(c, q, on_vector, g_t):
            if c == 0:
                part = raws[0][:, q // 2, :, NB * (q % 2) : NB * (q % 2 + 1)]
            else:
                part = raws[c][:, :, NB * q : NB * (q + 1)]
            src = part.rearrange("p t (c i) -> p c t i", i=4)
            dst = g_t[:, NB * (q % 2) : NB * (q % 2 + 1), :].rearrange("p (c i) t -> p c t i", i=4)
            if on_vector:
                nc.vector.tensor_copy(out=dst, in_=src)
            else:
                nc.scalar.copy(out=dst, in_=src)

        def quantise(g_t):
            wc = cod.tile([P, HALF], U32, tag="wc", name="wc", align_bytes=64)
            ws = cod.tile([P, HALF], U8, tag="ws", name="ws", align_bytes=64)
            nc.vector.quantize_mx(
                out=wc[:].bitcast(FP8X4), scales=ws[:], in_=g_t[:].rearrange("p c t -> p (c t)")
            )
            return wc, ws

        def multiply(c, hf, codes):
            h, kp = divmod(c, PASSES)
            wc, ws = codes
            for jj in range(2):
                nc.tensor.matmul_mx(
                    out=acc[(h, 2 * hf + jj)][:],
                    lhsT=xc[:, P * kp : P * (kp + 1)].bitcast(FP8X4),
                    lhsT_scale=xs[:, P * kp : P * (kp + 1)],
                    rhs=wc[:, NB * jj : NB * (jj + 1)].bitcast(FP8X4),
                    rhs_scale=ws[:, NB * jj : NB * (jj + 1)],
                    start=(kp == 0),
                    stop=(kp == PASSES - 1),
                )

        def quantise_and_multiply(c, hf, g_t):
            multiply(c, hf, quantise(g_t))

        hidden = {}

        def allocate_hidden():
            hid = act.tile([P, H * HID], BF16, tag="rows", name="hid", align_bytes=64)
            hg = act.tile([P, H * HID], BF16, tag="grouped", name="hg", align_bytes=64)
            hidden["rows"] = hid
            hidden["words"] = hid[:].bitcast(F32)
            hidden["grouped"] = hg
            hidden["grouped_words"] = hg[:].bitcast(F32).rearrange("p (g b u) -> p g b u", g=8, u=2)

        hc = const.tile([P, 8 * P], U32, name="hc", align_bytes=64)
        hs = const.tile([P, 8 * P], U8, name="hs", align_bytes=64)
        t_of = {}
        turned = {}

        def mix(g):
            h, j = divmod(g, 4)
            nc.vector.scalar_tensor_tensor(
                out=hidden["rows"][:, NB * g : NB * (g + 1)], in0=acc[(h, j)][:],
                scalar=w_f[:, h : h + 1], in1=t_of[h][:, NB * j : NB * (j + 1)], op0=ALU.mult, op1=ALU.add,
            )

        def turn(g, bank):
            ht = psum.tile([P, 2, P], F32, tag="%s%d" % (bank, g % 4), name="ht")
            for u in range(2):
                nc.tensor.transpose(ht[:, u, :], hidden["words"][:, 256 * g + u : 256 * (g + 1) : 2], ident_f[:])
            turned[g] = ht

        def collect(g):
            nc.scalar.copy(out=hidden["grouped_words"][:, g, :, :], in_=turned[g][:].rearrange("p u b -> p b u"))

        def quantise_hidden(g, n):
            nc.vector.quantize_mx(
                out=hc[:, P * g : P * (g + n)].bitcast(FP8X4), scales=hs[:, P * g : P * (g + n)],
                in_=hidden["grouped"][:, KP * g : KP * (g + n)],
            )

        acc2 = []

        def stage2_pass(g, j):
            wo = raws[NCH + g // 2]
            k = 4 * (g % 4)
            if g < 6:
                col = DOUT * (g % 2) + NB * j
            else:
                col = NB * (2 * j + g % 2)
            pcol = DOUT * (g // 4) + NB * j
            nc.tensor.matmul_mx(
                out=acc2[j][:],
                lhsT=hc[:, P * g : P * (g + 1)].bitcast(FP8X4),
                lhsT_scale=hs[:, P * g : P * (g + 1)],
                rhs=wo[:, col : col + NB].bitcast(FP8X4),
                rhs_scale=wos[k:P, pcol : pcol + NB],
                start=(g == 0),
                stop=(g == 7),
            )

        early_groups = {(14, 0): 0, (14, 1): 1, (15, 0): 2, (15, 1): 3}

        def early(c, slot):
            if (c, slot) in early_groups:
                for j in range(4):
                    stage2_pass(early_groups[(c, slot)], j)

        blocks = {}
        left = None
        for c in range(NCH):
            if c + RING - 1 < NCH + NPAIR:
                load(c + RING - 1)
            if c == PASSES:
                open_banks(1, "B")
            h0 = new_half()
            h1 = new_half()
            if c == 0:
                blocks[2] = spread_rows(ident_b, 8, "A")
                regroup(0, 1, False, h0)
                regroup(0, 0, True, h0)
                scalars_first()
                regroup(0, 3, False, h1)
                regroup(0, 2, True, h1)
                codes0 = quantise(h0)
                scalars_second()
                for j in range(4):
                    nc.scalar.copy(out=bout[:, NB * j : NB * (j + 1)], in_=blocks[2][j][:])
                blocks[0] = spread_rows(sel, 0, "B")
                codes1 = quantise(h1)
                t_of[0] = make_t(0, blocks[0])
                blocks[1] = spread_rows(sel, 4, "A")
                t_of[1] = make_t(1, blocks[1])
                prepare_x()
                open_banks(0, "A")
                multiply(0, 0, codes0)
                multiply(0, 1, codes1)
                allocate_hidden()
                continue
            light = c in V_LIGHT
            regroup(c, 1, False, h0)
            if light:
                regroup(c, 2, False, h1)
            regroup(c, 3, False, h1)
            regroup(c, 0, True, h0)
            if left is not None:
                quantise_and_multiply(c - 1, 1, left)
            early(c, 0)
            if c == PASSES:
                for g in range(4):
                    mix(g)
            if not light and c < NCH - 1:
                regroup(c, 2, True, h1)
            quantise_and_multiply(c, 0, h0)
            early(c, 1)
            if c == NCH - 1:
                regroup(c, 2, True, h1)
            left = h1
            if c == 9:
                for g in range(4):
                    turn(g, "A")
            if c == 10:
                for g in range(4):
                    collect(g)
            if c == 11:
                quantise_hidden(0, 4)
            if c == 12:
                for j in range(4):
                    a2 = psum.tile([P, NB], F32, tag="A%d" % j, name="acc2")
                    acc2.append(a2)

        mix(4)
        mix(5)
        turn(4, "B")
        turn(5, "B")
        collect(4)
        collect(5)
        quantise_and_multiply(NCH - 1, 1, left)
        quantise_hidden(4, 1)
        quantise_hidden(5, 1)
        mix(6)
        for j in range(4):
            stage2_pass(4, j)
        turn(6, "B")
        collect(6)
        mix(7)
        turn(7, "B")
        collect(7)
        quantise_hidden(6, 1)
        quantise_hidden(7, 1)
        for j in range(4):
            stage2_pass(5, j)
        o_sb = tpool.tile([P, DOUT], F32, tag="wide", name="o_sb")
        for j in range(4):
            stage2_pass(6, j)
            stage2_pass(7, j)
            nc.vector.tensor_tensor(
                out=o_sb[:, NB * j : NB * (j + 1)], in0=acc2[j][:], in1=bout[:, NB * j : NB * (j + 1)], op=ALU.add
            )
            nc.sync.dma_start(out=out[:, NB * j : NB * (j + 1)], in_=o_sb[:, NB * j : NB * (j + 1)])
